import numpy as np
import ml_dtypes


def mxq(x, axis, fmt="e4m3"):
    dtype, down = {"e4m3": (ml_dtypes.float8_e4m3fn, 7), "e5m2": (ml_dtypes.float8_e5m2, 14)}[fmt]
    v = np.moveaxis(np.asarray(x, np.float32).astype(ml_dtypes.bfloat16).astype(np.float64), axis, -1)
    blocks = v.reshape(v.shape[:-1] + (-1, 32))
    amax = np.abs(blocks).max(-1, keepdims=True)
    byte = np.maximum(np.where(amax > 0, np.frexp(amax)[1] - 1 + 127, 0) - down, 1)
    scale = np.exp2(byte - 127.0)
    codes = (blocks / scale).astype(np.float32).astype(dtype).astype(np.float64)
    return np.moveaxis((codes * scale).reshape(v.shape), -1, axis)


WIDE = False


def mx_kscale(k):
    if not WIDE:
        return np.ones(k)
    levels = np.array([20, -20, 10, -10, 0])
    a = np.random.permutation(np.resize(levels, k // 512 * 4)).reshape(k // 512, 4)
    idx = np.arange(k)
    return np.exp2(a[idx // 512, idx % 128 // 32])


BF16 = ml_dtypes.bfloat16


def bf(x):
    return np.asarray(x, np.float32).astype(BF16)


def f64(x):
    return np.asarray(x).astype(np.float64)


BATCH, IN_F, OUT_F = 8192, 512, 512


def softplus(v):
    return np.logaddexp(v, 0.0)


def setup_inputs():
    u = mx_kscale(OUT_F)
    xav = np.sqrt(2.0 / (IN_F + OUT_F))
    x = np.random.standard_normal((BATCH, IN_F))
    weight_mu = np.random.standard_normal((OUT_F, IN_F)) * xav / u[:, None]
    weight_rho = -3.0 + 0.3 * np.random.standard_normal((OUT_F, IN_F))
    bias_mu = 0.5 * np.random.standard_normal(OUT_F)
    bias_rho = -1.0 + 0.3 * np.random.standard_normal(OUT_F)
    weight_eps = np.random.standard_normal((OUT_F, IN_F)) / u[:, None]
    bias_eps = np.random.standard_normal(OUT_F)
    g = np.random.standard_normal((BATCH, OUT_F)) * np.exp2(np.random.randint(-12, 1, (BATCH, 1))) * 4.0 * u
    return {
        "x": bf(x),
        "weight_mu": bf(weight_mu),
        "weight_rho": bf(weight_rho),
        "bias_mu": bf(bias_mu),
        "bias_rho": bf(bias_rho),
        "weight_eps": bf(weight_eps),
        "bias_eps": bf(bias_eps),
        "grad_out": bf(g),
    }


def reference(x, weight_mu, weight_rho, bias_mu, bias_rho, weight_eps, bias_eps, grad_out):
    weight = f64(weight_mu) + softplus(f64(weight_rho)) * f64(weight_eps)
    return mxq(f64(grad_out), 1, "e5m2") @ mxq(weight, 0, "e4m3")

@@ -1,0 +1,234 @@
+from contextlib import ExitStack
+
+import concourse.mybir as mybir
+from concourse.masks import make_identity
+
+F32 = mybir.dt.float32
+BF16 = mybir.dt.bfloat16
+U32 = mybir.dt.uint32
+U8 = mybir.dt.uint8
+E4X4 = mybir.dt.float8_e4m3fn_x4
+E5X4 = mybir.dt.float8_e5m2_x4
+ALU = mybir.AluOpType
+ACT = mybir.ActivationFunctionType
+
+P = 128
+BATCH = 8192
+K = 512
+N = 512
+TILES = BATCH // P
+UNIT = 4
+UNITS = TILES // UNIT
+GROUP = 8
+W_PIECES = 4
+HEAD_UNITS = 7
+LEAD = 2
+LOADS = (8, 8, 8, 8, 16, 16)
+
+FLOPS = 2 * BATCH * K * N
+BYTES = BATCH * K * 2 + 3 * K * N * 2 + BATCH * N * 4
+
+
+def tile_bayesianlinear_t_kernel(
+    tc, x, weight_mu, weight_rho, bias_mu, bias_rho, weight_eps, bias_eps, grad_out, out
+):
+    nc = tc.nc
+    g_view = grad_out.rearrange("(p t) k -> p t k", t=TILES)
+    o_view = out.rearrange("(p t) i -> p t i", t=TILES)
+
+    with ExitStack() as ctx:
+        const = ctx.enter_context(tc.tile_pool(name="const", bufs=1))
+        gpool = ctx.enter_context(tc.tile_pool(name="gpool", bufs=1))
+        grpp = ctx.enter_context(tc.tile_pool(name="grpp", bufs=HEAD_UNITS))
+        codep = ctx.enter_context(tc.tile_pool(name="codep", bufs=4))
+        opool = ctx.enter_context(tc.tile_pool(name="opool", bufs=6))
+        ps_t = ctx.enter_context(tc.psum_pool(name="ps_t", bufs=4))
+        ps_o = ctx.enter_context(tc.psum_pool(name="ps_o", bufs=4))
+        ctx.enter_context(tc.manual_schedule())
+
+        def load_w(dram, name):
+            t = const.tile([P, 4 * N], BF16, name=name)
+            nc.sync.dma_start(
+                out=t[:].rearrange("p (u f) -> p u f", u=2),
+                in_=dram.rearrange("(u q e) c -> q u (e c)", u=2, q=P, e=2),
+            )
+            return t
+
+        g_of_tile = {}
+
+        def load_g(i):
+            t0 = sum(LOADS[:i])
+            cnt = LOADS[i]
+            t = gpool.tile([P, cnt * K], BF16, name="g%d" % i)
+            nc.sync.dma_start(
+                out=t[:], in_=g_view[:, t0 : t0 + cnt, :].rearrange("p t k -> p (t k)")
+            )
+            for j in range(cnt):
+                g_of_tile[t0 + j] = (t, j)
+
+        rho = load_w(weight_rho, "rho")
+        load_g(0)
+        eps = load_w(weight_eps, "eps")
+        mu = load_w(weight_mu, "mu")
+        for i in range(1, len(LOADS)):
+            load_g(i)
+
+        ident = const.tile([P, P], F32, name="ident")
+        make_identity(nc, ident[:])
+        ones = const.tile([P, 1], F32, name="ones")
+        nc.vector.memset(ones[:], 1.0)
+
+        neg_abs = const.tile([P, 4 * N], BF16, name="neg_abs")
+        acc_w = const.tile([P, 4 * N], F32, name="acc_w")
+        w_grp = const.tile([P, 4 * N], BF16, name="w_grp", align_bytes=64)
+        w_codes = const.tile([P, N], U32, name="w_codes", align_bytes=64)
+        w_scl = const.tile([P, N], U8, name="w_scl", align_bytes=64)
+        pc = N // W_PIECES
+
+        def piece(t, i):
+            return t[:].rearrange("p (t c) -> p t c", t=4)[:, :, i * pc : (i + 1) * pc]
+
+        def w_sub(i):
+            nc.vector.scalar_tensor_tensor(
+                out=piece(acc_w, i), in0=piece(rho, i), scalar=0.0, in1=piece(acc_w, i),
+                op0=ALU.max, op1=ALU.subtract,
+            )
+
+        def w_mul(i):
+            nc.vector.tensor_tensor(
+                out=piece(acc_w, i), in0=piece(acc_w, i), in1=piece(eps, i), op=ALU.mult
+            )
+
+        def w_add(i):
+            nc.vector.tensor_tensor(
+                out=w_grp[:, i * pc * 4 : (i + 1) * pc * 4].rearrange("p (c t) -> p c t", t=4),
+                in0=piece(acc_w, i).rearrange("p t c -> p c t"),
+                in1=piece(mu, i).rearrange("p t c -> p c t"),
+                op=ALU.add,
+            )
+
+        def w_quant(h):
+            half = N // 2
+            nc.vector.quantize_mx(
+                out=w_codes[:, h * half : (h + 1) * half].bitcast(E4X4),
+                scales=w_scl[:, h * half : (h + 1) * half],
+                in_=w_grp[:, h * half * 4 : (h + 1) * half * 4],
+            )
+
+        grp = {}
+        codes = {}
+        scl = {}
+        o_sb = {}
+
+        def copy_on(eng, dst, src):
+            if eng == "v":
+                nc.vector.tensor_copy(out=dst, in_=src)
+            else:
+                nc.scalar.copy(out=dst, in_=src)
+
+        def transposes(n, engs):
+            grp_n = grpp.tile([P, UNIT * K], BF16, name="grp", align_bytes=64)
+            grp[n] = grp_n
+            grp32 = grp_n[:].bitcast(F32)
+            for jj in range(UNIT // 2):
+                xt = ps_t.tile([P, 512], F32, name="xt")
+                for jl in range(2):
+                    g_t, j = g_of_tile[n * UNIT + jj * 2 + jl]
+                    g32 = g_t[:].bitcast(F32)
+                    for u in range(2):
+                        nc.tensor.transpose(
+                            xt[:, (jl * 2 + u) * P : (jl * 2 + u + 1) * P],
+                            g32[:, j * 256 + u * P : j * 256 + (u + 1) * P],
+                            ident[:],
+                        )
+                copy_on(
+                    engs[jj],
+                    grp32[:, jj * 512 : (jj + 1) * 512].rearrange(
+                        "p (j r u) -> p j r u", j=2, r=P, u=2
+                    ),
+                    xt[:].rearrange("p (j u r) -> p j r u", j=2, u=2, r=P),
+                )
+
+        def quantise(n):
+            codes_n = codep.tile([P, UNIT * P], U32, name="codes", align_bytes=64)
+            scl_n = codep.tile([P, UNIT * P], U8, name="scl", align_bytes=64)
+            codes[n] = codes_n
+            scl[n] = scl_n
+            nc.vector.quantize_mx(out=codes_n[:].bitcast(E5X4), scales=scl_n[:], in_=grp[n][:])
+
+        def passes(n, engs):
+            accs = []
+            for j in range(UNIT):
+                acc = ps_o.tile([P, N], F32, name="acc")
+                nc.tensor.matmul_mx(
+                    out=acc[:],
+                    lhsT=codes[n][:, j * P : (j + 1) * P].bitcast(E5X4),
+                    lhsT_scale=scl[n][:, j * P : (j + 1) * P],
+                    rhs=w_codes[:].bitcast(E4X4),
+                    rhs_scale=w_scl[:],
+                    start=True,
+                    stop=True,
+                )
+                accs.append(acc)
+            gidx, first = divmod(n * UNIT, GROUP)
+            if first == 0:
+                o_g = opool.tile([P, GROUP * N], F32, name="o_sb")
+                o_sb[gidx] = o_g
+            for j in range(UNIT):
+                copy_on(engs[j], o_sb[gidx][:, (first + j) * N : (first + j + 1) * N], accs[j][:])
+
+        def store(t0, cnt):
+            gidx, first = divmod(t0, GROUP)
+            nc.sync.dma_start(
+                out=o_view[:, t0 : t0 + cnt, :].rearrange("p t i -> p (t i)"),
+                in_=o_sb[gidx][:, first * N : (first + cnt) * N],
+            )
+
+        for i in range(W_PIECES):
+            nc.vector.scalar_tensor_tensor(
+                out=piece(neg_abs, i), in0=piece(rho, i), scalar=-1.0, in1=piece(rho, i),
+                op0=ALU.mult, op1=ALU.min,
+            )
+            nc.scalar.activation(out=piece(acc_w, i), in_=piece(neg_abs, i), func=ACT.Sigmoid)
+        transposes(0, "vv")
+        transposes(1, "vv")
+        quantise(0)
+        for i in range(W_PIECES):
+            nc.scalar.activation(
+                out=piece(acc_w, i), in_=piece(acc_w, i), func=ACT.Ln, scale=-1.0, bias=ones[:]
+            )
+        for n in range(2, HEAD_UNITS):
+            transposes(n, "ss")
+        w_sub(0)
+        w_sub(1)
+        w_mul(0)
+        w_mul(1)
+        w_add(0)
+        w_add(1)
+        w_sub(2)
+        w_sub(3)
+        w_mul(2)
+        w_mul(3)
+        w_add(2)
+        w_quant(0)
+        w_add(3)
+        quantise(1)
+        w_quant(1)
+
+        for n in range(UNITS):
+            if 1 <= n and n + 1 < UNITS:
+                quantise(n + 1)
+            nxt = n + LEAD
+            has_t = HEAD_UNITS <= nxt < UNITS
+            if has_t:
+                engs = "sssv" if n % 2 == 0 else "ssss"
+            else:
+                engs = "svsv" if n % 2 == 0 else "sssv"
+            passes(n, engs)
+            if has_t:
+                transposes(nxt, "vv")
+            t_end = (n + 1) * UNIT
+            if n in (0, 1, UNITS - 2, UNITS - 1):
+                store(t_end - UNIT, UNIT)
+            elif t_end % GROUP == 0:
+                store(t_end - GROUP, GROUP)

@@ -7,6 +7,7 @@ F32 = mybir.dt.float32
 BF16 = mybir.dt.bfloat16
 U32 = mybir.dt.uint32
 U8 = mybir.dt.uint8
+I32 = mybir.dt.int32
 E4X4 = mybir.dt.float8_e4m3fn_x4
 E5X4 = mybir.dt.float8_e5m2_x4
 ALU = mybir.AluOpType
@@ -21,7 +22,8 @@ UNIT = 4
 UNITS = TILES // UNIT
 GROUP = 8
 W_PIECES = 4
-HEAD_UNITS = 7
+HEAD_UNITS = 5
+SIGN_BITS = -2147450880
 LEAD = 2
 LOADS = (8, 8, 8, 8, 16, 16)
 
@@ -46,13 +48,11 @@ def tile_bayesianlinear_t_kernel(
         ps_o = ctx.enter_context(tc.psum_pool(name="ps_o", bufs=4))
         ctx.enter_context(tc.manual_schedule())
 
-        def load_w(dram, name):
-            t = const.tile([P, 4 * N], BF16, name=name)
+        def load_w_half(t, dram, u):
             nc.sync.dma_start(
-                out=t[:].rearrange("p (u f) -> p u f", u=2),
-                in_=dram.rearrange("(u q e) c -> q u (e c)", u=2, q=P, e=2),
+                out=t[:, u * 2 * N : (u + 1) * 2 * N],
+                in_=dram.rearrange("(u q e) c -> u q (e c)", u=2, q=P, e=2)[u],
             )
-            return t
 
         g_of_tile = {}
 
@@ -66,11 +66,17 @@ def tile_bayesianlinear_t_kernel(
             for j in range(cnt):
                 g_of_tile[t0 + j] = (t, j)
 
-        rho = load_w(weight_rho, "rho")
-        load_g(0)
-        eps = load_w(weight_eps, "eps")
-        mu = load_w(weight_mu, "mu")
-        for i in range(1, len(LOADS)):
+        rho = const.tile([P, 4 * N], BF16, name="rho")
+        eps = const.tile([P, 4 * N], BF16, name="eps")
+        mu = const.tile([P, 4 * N], BF16, name="mu")
+        for u in range(2):
+            load_w_half(rho, weight_rho, u)
+            load_w_half(eps, weight_eps, u)
+        nc.sync.dma_start(
+            out=mu[:].rearrange("p (u f) -> p u f", u=2),
+            in_=weight_mu.rearrange("(u q e) c -> q u (e c)", u=2, q=P, e=2),
+        )
+        for i in range(len(LOADS)):
             load_g(i)
 
         ident = const.tile([P, P], F32, name="ident")
@@ -80,6 +86,7 @@ def tile_bayesianlinear_t_kernel(
 
         neg_abs = const.tile([P, 4 * N], BF16, name="neg_abs")
         acc_w = const.tile([P, 4 * N], F32, name="acc_w")
+        base = const.tile([P, 4 * N], F32, name="base")
         w_grp = const.tile([P, 4 * N], BF16, name="w_grp", align_bytes=64)
         w_codes = const.tile([P, N], U32, name="w_codes", align_bytes=64)
         w_scl = const.tile([P, N], U8, name="w_scl", align_bytes=64)
@@ -88,10 +95,25 @@ def tile_bayesianlinear_t_kernel(
         def piece(t, i):
             return t[:].rearrange("p (t c) -> p t c", t=4)[:, :, i * pc : (i + 1) * pc]
 
-        def w_sub(i):
+        def half(t, u):
+            return t[:, u * 2 * N : (u + 1) * 2 * N]
+
+        def w_neg_abs(u):
+            nc.vector.tensor_scalar(
+                out=half(neg_abs, u).bitcast(I32), in0=half(rho, u).bitcast(I32),
+                scalar1=SIGN_BITS, scalar2=None, op0=ALU.bitwise_or,
+            )
+            nc.scalar.activation(out=half(acc_w, u), in_=half(neg_abs, u), func=ACT.Sigmoid)
+
+        def w_base1(u):
             nc.vector.scalar_tensor_tensor(
-                out=piece(acc_w, i), in0=piece(rho, i), scalar=0.0, in1=piece(acc_w, i),
-                op0=ALU.max, op1=ALU.subtract,
+                out=half(base, u), in0=half(rho, u), scalar=0.0, in1=half(eps, u),
+                op0=ALU.max, op1=ALU.mult,
+            )
+
+        def w_base2(u):
+            nc.vector.tensor_tensor(
+                out=half(base, u), in0=half(base, u), in1=half(mu, u), op=ALU.add
             )
 
         def w_mul(i):
@@ -99,12 +121,14 @@ def tile_bayesianlinear_t_kernel(
                 out=piece(acc_w, i), in0=piece(acc_w, i), in1=piece(eps, i), op=ALU.mult
             )
 
-        def w_add(i):
+        def w_fin(i):
             nc.vector.tensor_tensor(
-                out=w_grp[:, i * pc * 4 : (i + 1) * pc * 4].rearrange("p (c t) -> p c t", t=4),
-                in0=piece(acc_w, i).rearrange("p t c -> p c t"),
-                in1=piece(mu, i).rearrange("p t c -> p c t"),
-                op=ALU.add,
+                out=w_grp[:, i * pc * 4 : (i + 1) * pc * 4].rearrange(
+                    "p (c i t) -> p c t i", i=4, t=4
+                ),
+                in0=piece(base, i).rearrange("p t (c i) -> p c t i", i=4),
+                in1=piece(acc_w, i).rearrange("p t (c i) -> p c t i", i=4),
+                op=ALU.subtract,
             )
 
         def w_quant(h):
@@ -184,51 +208,47 @@ def tile_bayesianlinear_t_kernel(
                 in_=o_sb[gidx][:, first * N : (first + cnt) * N],
             )
 
-        for i in range(W_PIECES):
-            nc.vector.scalar_tensor_tensor(
-                out=piece(neg_abs, i), in0=piece(rho, i), scalar=-1.0, in1=piece(rho, i),
-                op0=ALU.mult, op1=ALU.min,
-            )
-            nc.scalar.activation(out=piece(acc_w, i), in_=piece(neg_abs, i), func=ACT.Sigmoid)
-        transposes(0, "vv")
-        transposes(1, "vv")
-        quantise(0)
+        w_neg_abs(0)
+        w_base1(0)
+        w_neg_abs(1)
+        w_base1(1)
+        w_base2(0)
+        w_base2(1)
         for i in range(W_PIECES):
             nc.scalar.activation(
                 out=piece(acc_w, i), in_=piece(acc_w, i), func=ACT.Ln, scale=-1.0, bias=ones[:]
             )
-        for n in range(2, HEAD_UNITS):
+        for n in range(HEAD_UNITS):
             transposes(n, "ss")
-        w_sub(0)
-        w_sub(1)
         w_mul(0)
         w_mul(1)
-        w_add(0)
-        w_add(1)
-        w_sub(2)
-        w_sub(3)
+        w_fin(0)
+        w_fin(1)
+        quantise(0)
         w_mul(2)
         w_mul(3)
-        w_add(2)
+        w_fin(2)
+        w_fin(3)
         w_quant(0)
-        w_add(3)
-        quantise(1)
         w_quant(1)
 
         for n in range(UNITS):
-            if 1 <= n and n + 1 < UNITS:
+            if n + 1 < UNITS:
                 quantise(n + 1)
             nxt = n + LEAD
             has_t = HEAD_UNITS <= nxt < UNITS
             if has_t:
                 engs = "sssv" if n % 2 == 0 else "ssss"
             else:
-                engs = "svsv" if n % 2 == 0 else "sssv"
+                engs = "svsv"
             passes(n, engs)
             if has_t:
                 transposes(nxt, "vv")
             t_end = (n + 1) * UNIT
-            if n in (0, 1, UNITS - 2, UNITS - 1):
+            if n == 0:
+                store(0, 2)
+                store(2, 2)
+            elif n in (1, UNITS - 2, UNITS - 1):
                 store(t_end - UNIT, UNIT)
             elif t_end % GROUP == 0:
                 store(t_end - GROUP, GROUP)

@@ -25,7 +25,7 @@ W_PIECES = 4
 HEAD_UNITS = 5
 SIGN_BITS = -2147450880
 LEAD = 2
-LOADS = (8, 8, 8, 8, 16, 16)
+LOADS = (8, 8, 16, 32)
 
 FLOPS = 2 * BATCH * K * N
 BYTES = BATCH * K * 2 + 3 * K * N * 2 + BATCH * N * 4
@@ -245,10 +245,7 @@ def tile_bayesianlinear_t_kernel(
             if has_t:
                 transposes(nxt, "vv")
             t_end = (n + 1) * UNIT
-            if n == 0:
-                store(0, 2)
-                store(2, 2)
-            elif n in (1, UNITS - 2, UNITS - 1):
+            if n in (0, 1, UNITS - 2, UNITS - 1):
                 store(t_end - UNIT, UNIT)
             elif t_end % GROUP == 0:
                 store(t_end - GROUP, GROUP)

@@ -150,11 +150,12 @@ def tile_bayesianlinear_t_kernel(
             else:
                 nc.scalar.copy(out=dst, in_=src)
 
-        def transposes(n, engs):
-            grp_n = grpp.tile([P, UNIT * K], BF16, name="grp", align_bytes=64)
-            grp[n] = grp_n
-            grp32 = grp_n[:].bitcast(F32)
-            for jj in range(UNIT // 2):
+        def transposes(n, engs, banks=(0, 1)):
+            if 0 in banks:
+                grp_n = grpp.tile([P, UNIT * K], BF16, name="grp", align_bytes=64)
+                grp[n] = grp_n
+            grp32 = grp[n][:].bitcast(F32)
+            for jj in banks:
                 xt = ps_t.tile([P, 512], F32, name="xt")
                 for jl in range(2):
                     g_t, j = g_of_tile[n * UNIT + jj * 2 + jl]
@@ -233,17 +234,19 @@ def tile_bayesianlinear_t_kernel(
         w_quant(1)
 
         for n in range(UNITS):
-            if n + 1 < UNITS:
-                quantise(n + 1)
             nxt = n + LEAD
             has_t = HEAD_UNITS <= nxt < UNITS
+            if has_t:
+                transposes(nxt, "vv", (0,))
+            if n + 1 < UNITS:
+                quantise(n + 1)
+            if has_t:
+                transposes(nxt, "vv", (1,))
             if has_t:
                 engs = "sssv" if n % 2 == 0 else "ssss"
             else:
                 engs = "svsv"
             passes(n, engs)
-            if has_t:
-                transposes(nxt, "vv")
             t_end = (n + 1) * UNIT
             if n in (0, 1, UNITS - 2, UNITS - 1):
                 store(t_end - UNIT, UNIT)

@@ -35,8 +35,6 @@ def tile_bayesianlinear_t_kernel(
     tc, x, weight_mu, weight_rho, bias_mu, bias_rho, weight_eps, bias_eps, grad_out, out
 ):
     nc = tc.nc
-    g_view = grad_out.rearrange("(p t) k -> p t k", t=TILES)
-    o_view = out.rearrange("(p t) i -> p t i", t=TILES)
 
     with ExitStack() as ctx:
         const = ctx.enter_context(tc.tile_pool(name="const", bufs=1))
@@ -55,16 +53,19 @@ def tile_bayesianlinear_t_kernel(
             )
 
         g_of_tile = {}
+        block_of_tile = {}
 
         def load_g(i):
             t0 = sum(LOADS[:i])
             cnt = LOADS[i]
             t = gpool.tile([P, cnt * K], BF16, name="g%d" % i)
             nc.sync.dma_start(
-                out=t[:], in_=g_view[:, t0 : t0 + cnt, :].rearrange("p t k -> p (t k)")
+                out=t[:],
+                in_=grad_out[t0 * P : (t0 + cnt) * P, :].rearrange("(p t) k -> p (t k)", t=cnt),
             )
             for j in range(cnt):
                 g_of_tile[t0 + j] = (t, j)
+                block_of_tile[t0 + j] = (t0, cnt)
 
         rho = const.tile([P, 4 * N], BF16, name="rho")
         eps = const.tile([P, 4 * N], BF16, name="eps")
@@ -204,8 +205,10 @@ def tile_bayesianlinear_t_kernel(
 
         def store(t0, cnt):
             gidx, first = divmod(t0, GROUP)
+            b0, bcnt = block_of_tile[t0]
+            o_block = out[b0 * P : (b0 + bcnt) * P, :].rearrange("(p t) i -> p t i", t=bcnt)
             nc.sync.dma_start(
-                out=o_view[:, t0 : t0 + cnt, :].rearrange("p t i -> p (t i)"),
+                out=o_block[:, t0 - b0 : t0 - b0 + cnt, :].rearrange("p t i -> p (t i)"),
                 in_=o_sb[gidx][:, first * N : (first + cnt) * N],
             )
 

@@ -20,7 +20,7 @@ N = 512
 TILES = BATCH // P
 UNIT = 4
 UNITS = TILES // UNIT
-GROUP = 8
+STORES = (8, 8, 8, 8, 8, 12, 12)
 W_PIECES = 4
 HEAD_UNITS = 5
 SIGN_BITS = -2147450880
@@ -41,7 +41,7 @@ def tile_bayesianlinear_t_kernel(
         gpool = ctx.enter_context(tc.tile_pool(name="gpool", bufs=1))
         grpp = ctx.enter_context(tc.tile_pool(name="grpp", bufs=HEAD_UNITS))
         codep = ctx.enter_context(tc.tile_pool(name="codep", bufs=4))
-        opool = ctx.enter_context(tc.tile_pool(name="opool", bufs=6))
+        opool = ctx.enter_context(tc.tile_pool(name="opool", bufs=4))
         ps_t = ctx.enter_context(tc.psum_pool(name="ps_t", bufs=4))
         ps_o = ctx.enter_context(tc.psum_pool(name="ps_o", bufs=4))
         ctx.enter_context(tc.manual_schedule())
@@ -144,6 +144,10 @@ def tile_bayesianlinear_t_kernel(
         codes = {}
         scl = {}
         o_sb = {}
+        store_of_tile = {}
+        for i in range(len(STORES)):
+            for j in range(STORES[i]):
+                store_of_tile[sum(STORES[:i]) + j] = (sum(STORES[:i]), STORES[i])
 
         def copy_on(eng, dst, src):
             if eng == "v":
@@ -196,20 +200,20 @@ def tile_bayesianlinear_t_kernel(
                     stop=True,
                 )
                 accs.append(acc)
-            gidx, first = divmod(n * UNIT, GROUP)
+            s0, cnt = store_of_tile[n * UNIT]
+            first = n * UNIT - s0
             if first == 0:
-                o_g = opool.tile([P, GROUP * N], F32, name="o_sb")
-                o_sb[gidx] = o_g
+                o_g = opool.tile([P, cnt * N], F32, name="o_sb")
+                o_sb[s0] = o_g
             for j in range(UNIT):
-                copy_on(engs[j], o_sb[gidx][:, (first + j) * N : (first + j + 1) * N], accs[j][:])
+                copy_on(engs[j], o_sb[s0][:, (first + j) * N : (first + j + 1) * N], accs[j][:])
 
         def store(t0, cnt):
-            gidx, first = divmod(t0, GROUP)
             b0, bcnt = block_of_tile[t0]
             o_block = out[b0 * P : (b0 + bcnt) * P, :].rearrange("(p t) i -> p t i", t=bcnt)
             nc.sync.dma_start(
                 out=o_block[:, t0 - b0 : t0 - b0 + cnt, :].rearrange("p t i -> p (t i)"),
-                in_=o_sb[gidx][:, first * N : (first + cnt) * N],
+                in_=o_sb[t0][:],
             )
 
         w_neg_abs(0)
@@ -251,7 +255,6 @@ def tile_bayesianlinear_t_kernel(
                 engs = "svsv"
             passes(n, engs)
             t_end = (n + 1) * UNIT
-            if n in (0, 1, UNITS - 2, UNITS - 1):
-                store(t_end - UNIT, UNIT)
-            elif t_end % GROUP == 0:
-                store(t_end - GROUP, GROUP)
+            s0, cnt = store_of_tile[t_end - 1]
+            if t_end == s0 + cnt:
+                store(s0, cnt)

@@ -21,6 +21,7 @@ TILES = BATCH // P
 UNIT = 4
 UNITS = TILES // UNIT
 STORES = (8, 8, 8, 8, 8, 12, 12)
+SCALAR_STORES = (8, 24, 52)
 W_PIECES = 4
 HEAD_UNITS = 5
 SIGN_BITS = -2147450880
@@ -211,7 +212,8 @@ def tile_bayesianlinear_t_kernel(
         def store(t0, cnt):
             b0, bcnt = block_of_tile[t0]
             o_block = out[b0 * P : (b0 + bcnt) * P, :].rearrange("(p t) i -> p t i", t=bcnt)
-            nc.sync.dma_start(
+            queue = nc.scalar if t0 in SCALAR_STORES else nc.sync
+            queue.dma_start(
                 out=o_block[:, t0 - b0 : t0 - b0 + cnt, :].rearrange("p t i -> p (t i)"),
                 in_=o_sb[t0][:],
             )

from contextlib import ExitStack

import concourse.mybir as mybir
from concourse.masks import make_identity

F32 = mybir.dt.float32
BF16 = mybir.dt.bfloat16
U32 = mybir.dt.uint32
U8 = mybir.dt.uint8
I32 = mybir.dt.int32
E4X4 = mybir.dt.float8_e4m3fn_x4
E5X4 = mybir.dt.float8_e5m2_x4
ALU = mybir.AluOpType
ACT = mybir.ActivationFunctionType

P = 128
BATCH = 8192
K = 512
N = 512
TILES = BATCH // P
UNIT = 4
UNITS = TILES // UNIT
STORES = (8, 8, 8, 8, 8, 12, 12)
SCALAR_STORES = (8, 24, 52)
W_PIECES = 4
HEAD_UNITS = 5
SIGN_BITS = -2147450880
LEAD = 2
LOADS = (8, 8, 16, 32)

FLOPS = 2 * BATCH * K * N
BYTES = BATCH * K * 2 + 3 * K * N * 2 + BATCH * N * 4


def tile_bayesianlinear_t_kernel(
    tc, x, weight_mu, weight_rho, bias_mu, bias_rho, weight_eps, bias_eps, grad_out, out
):
    nc = tc.nc

    with ExitStack() as ctx:
        const = ctx.enter_context(tc.tile_pool(name="const", bufs=1))
        gpool = ctx.enter_context(tc.tile_pool(name="gpool", bufs=1))
        grpp = ctx.enter_context(tc.tile_pool(name="grpp", bufs=HEAD_UNITS))
        codep = ctx.enter_context(tc.tile_pool(name="codep", bufs=4))
        opool = ctx.enter_context(tc.tile_pool(name="opool", bufs=4))
        ps_t = ctx.enter_context(tc.psum_pool(name="ps_t", bufs=4))
        ps_o = ctx.enter_context(tc.psum_pool(name="ps_o", bufs=4))
        ctx.enter_context(tc.manual_schedule())

        def load_w_half(t, dram, u):
            nc.sync.dma_start(
                out=t[:, u * 2 * N : (u + 1) * 2 * N],
                in_=dram.rearrange("(u q e) c -> u q (e c)", u=2, q=P, e=2)[u],
            )

        g_of_tile = {}
        block_of_tile = {}

        def load_g(i):
            t0 = sum(LOADS[:i])
            cnt = LOADS[i]
            t = gpool.tile([P, cnt * K], BF16, name="g%d" % i)
            nc.sync.dma_start(
                out=t[:],
                in_=grad_out[t0 * P : (t0 + cnt) * P, :].rearrange("(p t) k -> p (t k)", t=cnt),
            )
            for j in range(cnt):
                g_of_tile[t0 + j] = (t, j)
                block_of_tile[t0 + j] = (t0, cnt)

        rho = const.tile([P, 4 * N], BF16, name="rho")
        eps = const.tile([P, 4 * N], BF16, name="eps")
        mu = const.tile([P, 4 * N], BF16, name="mu")
        for u in range(2):
            load_w_half(rho, weight_rho, u)
            load_w_half(eps, weight_eps, u)
        nc.sync.dma_start(
            out=mu[:].rearrange("p (u f) -> p u f", u=2),
            in_=weight_mu.rearrange("(u q e) c -> q u (e c)", u=2, q=P, e=2),
        )
        for i in range(len(LOADS)):
            load_g(i)

        ident = const.tile([P, P], F32, name="ident")
        make_identity(nc, ident[:])
        ones = const.tile([P, 1], F32, name="ones")
        nc.vector.memset(ones[:], 1.0)

        neg_abs = const.tile([P, 4 * N], BF16, name="neg_abs")
        acc_w = const.tile([P, 4 * N], F32, name="acc_w")
        base = const.tile([P, 4 * N], F32, name="base")
        w_grp = const.tile([P, 4 * N], BF16, name="w_grp", align_bytes=64)
        w_codes = const.tile([P, N], U32, name="w_codes", align_bytes=64)
        w_scl = const.tile([P, N], U8, name="w_scl", align_bytes=64)
        pc = N // W_PIECES

        def piece(t, i):
            return t[:].rearrange("p (t c) -> p t c", t=4)[:, :, i * pc : (i + 1) * pc]

        def half(t, u):
            return t[:, u * 2 * N : (u + 1) * 2 * N]

        def w_neg_abs(u):
            nc.vector.tensor_scalar(
                out=half(neg_abs, u).bitcast(I32), in0=half(rho, u).bitcast(I32),
                scalar1=SIGN_BITS, scalar2=None, op0=ALU.bitwise_or,
            )
            nc.scalar.activation(out=half(acc_w, u), in_=half(neg_abs, u), func=ACT.Sigmoid)

        def w_base1(u):
            nc.vector.scalar_tensor_tensor(
                out=half(base, u), in0=half(rho, u), scalar=0.0, in1=half(eps, u),
                op0=ALU.max, op1=ALU.mult,
            )

        def w_base2(u):
            nc.vector.tensor_tensor(
                out=half(base, u), in0=half(base, u), in1=half(mu, u), op=ALU.add
            )

        def w_mul(i):
            nc.vector.tensor_tensor(
                out=piece(acc_w, i), in0=piece(acc_w, i), in1=piece(eps, i), op=ALU.mult
            )

        def w_fin(i):
            nc.vector.tensor_tensor(
                out=w_grp[:, i * pc * 4 : (i + 1) * pc * 4].rearrange(
                    "p (c i t) -> p c t i", i=4, t=4
                ),
                in0=piece(base, i).rearrange("p t (c i) -> p c t i", i=4),
                in1=piece(acc_w, i).rearrange("p t (c i) -> p c t i", i=4),
                op=ALU.subtract,
            )

        def w_quant(h):
            half = N // 2
            nc.vector.quantize_mx(
                out=w_codes[:, h * half : (h + 1) * half].bitcast(E4X4),
                scales=w_scl[:, h * half : (h + 1) * half],
                in_=w_grp[:, h * half * 4 : (h + 1) * half * 4],
            )

        grp = {}
        codes = {}
        scl = {}
        o_sb = {}
        store_of_tile = {}
        for i in range(len(STORES)):
            for j in range(STORES[i]):
                store_of_tile[sum(STORES[:i]) + j] = (sum(STORES[:i]), STORES[i])

        def copy_on(eng, dst, src):
            if eng == "v":
                nc.vector.tensor_copy(out=dst, in_=src)
            else:
                nc.scalar.copy(out=dst, in_=src)

        def transposes(n, engs, banks=(0, 1)):
            if 0 in banks:
                grp_n = grpp.tile([P, UNIT * K], BF16, name="grp", align_bytes=64)
                grp[n] = grp_n
            grp32 = grp[n][:].bitcast(F32)
            for jj in banks:
                xt = ps_t.tile([P, 512], F32, name="xt")
                for jl in range(2):
                    g_t, j = g_of_tile[n * UNIT + jj * 2 + jl]
                    g32 = g_t[:].bitcast(F32)
                    for u in range(2):
                        nc.tensor.transpose(
                            xt[:, (jl * 2 + u) * P : (jl * 2 + u + 1) * P],
                            g32[:, j * 256 + u * P : j * 256 + (u + 1) * P],
                            ident[:],
                        )
                copy_on(
                    engs[jj],
                    grp32[:, jj * 512 : (jj + 1) * 512].rearrange(
                        "p (j r u) -> p j r u", j=2, r=P, u=2
                    ),
                    xt[:].rearrange("p (j u r) -> p j r u", j=2, u=2, r=P),
                )

        def quantise(n):
            codes_n = codep.tile([P, UNIT * P], U32, name="codes", align_bytes=64)
            scl_n = codep.tile([P, UNIT * P], U8, name="scl", align_bytes=64)
            codes[n] = codes_n
            scl[n] = scl_n
            nc.vector.quantize_mx(out=codes_n[:].bitcast(E5X4), scales=scl_n[:], in_=grp[n][:])

        def passes(n, engs):
            accs = []
            for j in range(UNIT):
                acc = ps_o.tile([P, N], F32, name="acc")
                nc.tensor.matmul_mx(
                    out=acc[:],
                    lhsT=codes[n][:, j * P : (j + 1) * P].bitcast(E5X4),
                    lhsT_scale=scl[n][:, j * P : (j + 1) * P],
                    rhs=w_codes[:].bitcast(E4X4),
                    rhs_scale=w_scl[:],
                    start=True,
                    stop=True,
                )
                accs.append(acc)
            s0, cnt = store_of_tile[n * UNIT]
            first = n * UNIT - s0
            if first == 0:
                o_g = opool.tile([P, cnt * N], F32, name="o_sb")
                o_sb[s0] = o_g
            for j in range(UNIT):
                copy_on(engs[j], o_sb[s0][:, (first + j) * N : (first + j + 1) * N], accs[j][:])

        def store(t0, cnt):
            b0, bcnt = block_of_tile[t0]
            o_block = out[b0 * P : (b0 + bcnt) * P, :].rearrange("(p t) i -> p t i", t=bcnt)
            queue = nc.scalar if t0 in SCALAR_STORES else nc.sync
            queue.dma_start(
                out=o_block[:, t0 - b0 : t0 - b0 + cnt, :].rearrange("p t i -> p (t i)"),
                in_=o_sb[t0][:],
            )

        w_neg_abs(0)
        w_base1(0)
        w_neg_abs(1)
        w_base1(1)
        w_base2(0)
        w_base2(1)
        for i in range(W_PIECES):
            nc.scalar.activation(
                out=piece(acc_w, i), in_=piece(acc_w, i), func=ACT.Ln, scale=-1.0, bias=ones[:]
            )
        for n in range(HEAD_UNITS):
            transposes(n, "ss")
        w_mul(0)
        w_mul(1)
        w_fin(0)
        w_fin(1)
        quantise(0)
        w_mul(2)
        w_mul(3)
        w_fin(2)
        w_fin(3)
        w_quant(0)
        w_quant(1)

        for n in range(UNITS):
            nxt = n + LEAD
            has_t = HEAD_UNITS <= nxt < UNITS
            if has_t:
                transposes(nxt, "vv", (0,))
            if n + 1 < UNITS:
                quantise(n + 1)
            if has_t:
                transposes(nxt, "vv", (1,))
            if has_t:
                engs = "sssv" if n % 2 == 0 else "ssss"
            else:
                engs = "svsv"
            passes(n, engs)
            t_end = (n + 1) * UNIT
            s0, cnt = store_of_tile[t_end - 1]
            if t_end == s0 + cnt:
                store(s0, cnt)
